import numpy as np
import ml_dtypes


def mxq(x, axis, fmt="e4m3"):
    dtype, down = {"e4m3": (ml_dtypes.float8_e4m3fn, 7), "e5m2": (ml_dtypes.float8_e5m2, 14)}[fmt]
    v = np.moveaxis(np.asarray(x, np.float32).astype(ml_dtypes.bfloat16).astype(np.float64), axis, -1)
    blocks = v.reshape(v.shape[:-1] + (-1, 32))
    amax = np.abs(blocks).max(-1, keepdims=True)
    byte = np.maximum(np.where(amax > 0, np.frexp(amax)[1] - 1 + 127, 0) - down, 1)
    scale = np.exp2(byte - 127.0)
    codes = (blocks / scale).astype(np.float32).astype(dtype).astype(np.float64)
    return np.moveaxis((codes * scale).reshape(v.shape), -1, axis)


WIDE = False


def mx_kscale(k):
    if not WIDE:
        return np.ones(k)
    levels = np.array([10, -10, 5, -5, 0])
    a = np.random.permutation(np.resize(levels, k // 512 * 4)).reshape(k // 512, 4)
    idx = np.arange(k)
    return np.exp2(a[idx // 512, idx % 128 // 32])


BF16 = ml_dtypes.bfloat16


def bf(x):
    return np.asarray(x, np.float32).astype(BF16)


def f64(x):
    return np.asarray(x).astype(np.float64)


S, D, H, HD, CQ, CKV, O = 1024, 2048, 16, 128, 96, 512, 2048
E = H * HD
ROPE_BASE = 10000.0


def rope(xh, cos, sin):
    half = xh.shape[-1] // 2
    x1, x2 = xh[..., :half], xh[..., half:]
    rot = np.concatenate([-x2, x1], axis=-1)
    return xh * cos[:, None, :] + rot * sin[:, None, :]


def setup_inputs():
    s, t = mx_kscale(D), mx_kscale(CKV)
    pos = np.arange(S, dtype=np.float64)[:, None]
    inv_freq = 1.0 / (ROPE_BASE ** (np.arange(0, HD, 2, dtype=np.float64) / HD))
    ang = pos * inv_freq[None, :]
    return {"x": bf(np.random.standard_normal((S, D)) * s[None, :]),
            "rope_cos": bf(np.concatenate([np.cos(ang), np.cos(ang)], axis=-1)),
            "rope_sin": bf(np.concatenate([np.sin(ang), np.sin(ang)], axis=-1)),
            "wkv_down": bf(np.random.standard_normal((CKV, D)) / np.sqrt(D) * t[:, None] / s[None, :]),
            "bkv_down": bf(np.random.standard_normal(CKV) * 0.3 * t),
            "wk_up": bf(np.random.standard_normal((E, CKV)) / np.sqrt(CKV) / t[None, :]),
            "bk_up": bf(np.random.standard_normal(E) * 0.3),
            "wv_up": bf(np.random.standard_normal((E, CKV)) / np.sqrt(CKV) / t[None, :]),
            "bv_up": bf(np.random.standard_normal(E) * 0.3)}


def reference(x, rope_cos, rope_sin, wkv_down, bkv_down, wk_up, bk_up, wv_up, bv_up):
    c_kv = (mxq(f64(x), 1, "e4m3") @ mxq(f64(wkv_down), 1, "e4m3").T) + f64(bkv_down)
    cq = mxq(c_kv, 1, "e4m3")
    k = ((cq @ mxq(f64(wk_up), 1, "e4m3").T) + f64(bk_up)).reshape(S, H, HD)
    v = ((cq @ mxq(f64(wv_up), 1, "e4m3").T) + f64(bv_up)).reshape(S, H, HD)
    return rope(k, f64(rope_cos), f64(rope_sin)), v

@@ -1,0 +1,292 @@
+from contextlib import ExitStack
+
+import concourse.mybir as mybir
+from concourse.masks import make_identity
+
+F32 = mybir.dt.float32
+BF16 = mybir.dt.bfloat16
+U32 = mybir.dt.uint32
+U8 = mybir.dt.uint8
+FP8X4 = mybir.dt.float8_e4m3fn_x4
+ADD = mybir.AluOpType.add
+SUBTRACT = mybir.AluOpType.subtract
+MULT = mybir.AluOpType.mult
+IDENTITY = mybir.ActivationFunctionType.Identity
+
+P = 128
+PACK = 4
+K_PASS = P * PACK
+WORDS = K_PASS // 2
+BANK = 512
+
+S, D, CKV, HEADS, HEAD_DIM = 1024, 2048, 512, 16, 128
+E = HEADS * HEAD_DIM
+HALF_DIM = HEAD_DIM // 2
+S_TILES = S // P
+S_HALVES = S // BANK
+TILES_PER_HALF = BANK // P
+D_PASSES = D // K_PASS
+E_CHUNKS = E // BANK
+HEADS_PER_CHUNK = BANK // HEAD_DIM
+
+FLOPS = 2 * S * D * CKV + 2 * 2 * S * CKV * E
+
+
+def quantise_512_rows(nc, banks, stage, identity, copies, raw_words, codes, scales):
+    grouped = stage.tile([P, 4 * P, PACK], BF16, tag="grouped", align_bytes=64)
+    grouped_words = grouped[:].bitcast(F32)
+    for pair in range(2):
+        bank = banks.tile([P, 2, 2, P], F32, tag="turned", bufs=4)
+        for r in range(2):
+            for u in range(2):
+                nc.tensor.transpose(
+                    bank[:, r, u, :], raw_words[:, 2 * pair + r, u * P : (u + 1) * P], identity[:]
+                )
+        copies[pair](
+            out=grouped_words[:, 2 * pair * P : 2 * (pair + 1) * P, :].rearrange(
+                "p (r row) u -> p r row u", r=2
+            ),
+            in_=bank[:].rearrange("p r u row -> p r row u"),
+        )
+    nc.vector.quantize_mx(
+        out=codes.bitcast(FP8X4), scales=scales, in_=grouped[:].rearrange("p row t -> p (row t)")
+    )
+
+
+def tile_selfattention_pa_kernel(
+    tc, x, rope_cos, rope_sin, wkv_down, bkv_down, wk_up, bk_up, wv_up, bv_up, out_0, out_1
+):
+    nc = tc.nc
+    with ExitStack() as pools:
+        keep = pools.enter_context(tc.tile_pool(name="keep", bufs=1))
+        stage = pools.enter_context(tc.tile_pool(name="stage", bufs=4))
+        work = pools.enter_context(tc.tile_pool(name="work", bufs=2))
+        results = pools.enter_context(tc.tile_pool(name="results", bufs=4))
+        banks = pools.enter_context(tc.psum_pool(name="banks", bufs=2))
+
+        identity = keep.tile([P, P], F32)
+        make_identity(nc, identity[:])
+
+        wkv_raw = keep.tile([P, PACK, D], BF16)
+        wkv_rows = wkv_down.rearrange("(u p e) d -> p u e d", u=2, e=2)
+        for u in range(2):
+            nc.sync.dma_start(out=wkv_raw[:, 2 * u : 2 * u + 2, :], in_=wkv_rows[:, u])
+        bkv = keep.tile([P, PACK], BF16)
+        nc.sync.dma_start(
+            out=bkv[:].rearrange("p (u e) -> p u e", u=2),
+            in_=bkv_down.rearrange("(u p e) -> p u e", u=2, e=2),
+        )
+
+        x_raw = keep.tile([P, S_TILES, D], BF16)
+        x_rows = x.rearrange("(j p) d -> p j d", p=P)
+        wk_raw = keep.tile([P, HEADS, CKV], BF16)
+        wk_rows = wk_up.rearrange("(h p) c -> p h c", p=P)
+        wv_raw = keep.tile([P, HEADS, CKV], BF16)
+        wv_rows = wv_up.rearrange("(h p) c -> p h c", p=P)
+
+        def load_x_half(half):
+            for j in range(half * TILES_PER_HALF, (half + 1) * TILES_PER_HALF, 2):
+                nc.sync.dma_start(out=x_raw[:, j : j + 2, :], in_=x_rows[:, j : j + 2, :])
+
+        def load_up_weights(q):
+            heads = slice(q * HEADS_PER_CHUNK, (q + 1) * HEADS_PER_CHUNK)
+            nc.sync.dma_start(out=wk_raw[:, heads, :], in_=wk_rows[:, heads, :])
+            nc.sync.dma_start(out=wv_raw[:, heads, :], in_=wv_rows[:, heads, :])
+
+        load_x_half(0)
+        load_up_weights(0)
+        bk_bf16 = keep.tile([P, HEADS], BF16)
+        with nc.allow_non_contiguous_dma(reason="a 4 KiB bias, one element to a partition"):
+            nc.sync.dma_start(out=bk_bf16[:], in_=bk_up.rearrange("(h d) -> d h", d=HEAD_DIM))
+        tables = keep.tile([P, S_TILES, 2, HEAD_DIM], BF16)
+        cos_rows = rope_cos.rearrange("(j p) d -> p j d", p=P)
+        sin_rows = rope_sin.rearrange("(j p) d -> p j d", p=P)
+        nc.sync.dma_start(out=tables[:, :, 0, :], in_=cos_rows)
+        nc.sync.dma_start(out=tables[:, :, 1, :HALF_DIM], in_=sin_rows[:, :, HALF_DIM:])
+        nc.sync.dma_start(out=tables[:, :, 1, HALF_DIM:], in_=sin_rows[:, :, :HALF_DIM])
+        bv_all = keep.tile([P, E], BF16)
+        nc.sync.dma_start(out=bv_all[:], in_=bv_up.partition_broadcast(P))
+        for q in range(1, E_CHUNKS):
+            load_up_weights(q)
+        load_x_half(1)
+
+        bk = keep.tile([P, HEADS], F32)
+        nc.vector.tensor_copy(out=bk[:], in_=bk_bf16[:])
+
+        wkv_codes = keep.tile([P, D_PASSES, CKV], U32, align_bytes=64)
+        wkv_scales = keep.tile([P, D_PASSES, CKV], U8, align_bytes=64)
+        x_codes = keep.tile([P, D_PASSES, S], U32, align_bytes=64)
+        x_scales = keep.tile([P, D_PASSES, S], U8, align_bytes=64)
+        c_codes = keep.tile([P, S], U32, align_bytes=64)
+        c_scales = keep.tile([P, S], U8, align_bytes=64)
+        wk_codes = keep.tile([P, E], U32, align_bytes=64)
+        wk_scales = keep.tile([P, E], U8, align_bytes=64)
+        wv_codes = keep.tile([P, E], U32, align_bytes=64)
+        wv_scales = keep.tile([P, E], U8, align_bytes=64)
+
+        wkv_words = wkv_raw[:].bitcast(F32)
+        x_words = x_raw[:].bitcast(F32)
+        wk_words = wk_raw[:].bitcast(F32)
+        wv_words = wv_raw[:].bitcast(F32)
+
+        shared_copies = (nc.scalar.copy, nc.vector.tensor_copy)
+        scalar_copies = (nc.scalar.copy, nc.scalar.copy)
+
+        def quantise_x_half(half):
+            tiles = slice(half * TILES_PER_HALF, (half + 1) * TILES_PER_HALF)
+            cols = slice(half * BANK, (half + 1) * BANK)
+            copies = shared_copies if half == 0 else scalar_copies
+            for g in range(D_PASSES):
+                quantise_512_rows(
+                    nc, banks, stage, identity, copies,
+                    x_words[:, tiles, g * WORDS : (g + 1) * WORDS],
+                    x_codes[:, g, cols], x_scales[:, g, cols],
+                )
+
+        def quantise_up_weight(q, words, codes, scales):
+            heads = slice(q * HEADS_PER_CHUNK, (q + 1) * HEADS_PER_CHUNK)
+            cols = slice(q * BANK, (q + 1) * BANK)
+            quantise_512_rows(
+                nc, banks, stage, identity, scalar_copies,
+                words[:, heads, :], codes[:, cols], scales[:, cols],
+            )
+
+        def compress_half(half):
+            c_grouped = stage.tile([P, BANK, PACK], BF16, tag="grouped", align_bytes=64)
+            for jj in range(TILES_PER_HALF):
+                pos = slice((half * TILES_PER_HALF + jj) * P, (half * TILES_PER_HALF + jj + 1) * P)
+                c_bank = banks.tile([P, PACK, P], F32, tag="for_vector")
+                for t in range(PACK):
+                    rows = slice(t * P, (t + 1) * P)
+                    for g in range(D_PASSES):
+                        nc.tensor.matmul_mx(
+                            out=c_bank[:, t, :],
+                            lhsT=wkv_codes[:, g, rows].bitcast(FP8X4),
+                            lhsT_scale=wkv_scales[:, g, rows],
+                            rhs=x_codes[:, g, pos].bitcast(FP8X4),
+                            rhs_scale=x_scales[:, g, pos],
+                            start=(g == 0),
+                            stop=(g == D_PASSES - 1),
+                        )
+                nc.vector.tensor_tensor(
+                    out=c_grouped[:, jj * P : (jj + 1) * P, :],
+                    in0=c_bank[:].rearrange("p t s -> p s t"),
+                    in1=bkv[:].unsqueeze(1).to_broadcast([P, P, PACK]),
+                    op=ADD,
+                )
+            cols = slice(half * BANK, (half + 1) * BANK)
+            nc.vector.quantize_mx(
+                out=c_codes[:, cols].bitcast(FP8X4),
+                scales=c_scales[:, cols],
+                in_=c_grouped[:].rearrange("p s t -> p (s t)"),
+            )
+
+        def project_keys(half, q):
+            pos = slice(half * BANK, (half + 1) * BANK)
+            kT = work.tile([P, HEADS_PER_CHUNK, BANK], F32, tag="kT")
+            for hh in range(HEADS_PER_CHUNK):
+                h = q * HEADS_PER_CHUNK + hh
+                cols = slice(h * HEAD_DIM, (h + 1) * HEAD_DIM)
+                kT_bank = banks.tile([P, BANK], F32, tag="for_scalar")
+                nc.tensor.matmul_mx(
+                    out=kT_bank[:],
+                    lhsT=wk_codes[:, cols].bitcast(FP8X4),
+                    lhsT_scale=wk_scales[:, cols],
+                    rhs=c_codes[:, pos].bitcast(FP8X4),
+                    rhs_scale=c_scales[:, pos],
+                    start=True,
+                    stop=True,
+                )
+                nc.scalar.activation(
+                    out=kT[:, hh, :], in_=kT_bank[:], func=IDENTITY, bias=bk[:, h : h + 1], scale=1.0
+                )
+            return kT
+
+        def rotate_keys(half, q, kT):
+            heads = slice(q * HEADS_PER_CHUNK, (q + 1) * HEADS_PER_CHUNK)
+            shape = [P, 2, HEADS_PER_CHUNK, HEAD_DIM]
+            for first in range(half * TILES_PER_HALF, (half + 1) * TILES_PER_HALF, 2):
+                products = results.tile([P, 2, 2, HEADS_PER_CHUNK, HEAD_DIM], F32, tag="products")
+                for r in range(2):
+                    j = first + r
+                    jj = j - half * TILES_PER_HALF
+                    k_bank = banks.tile([P, HEADS_PER_CHUNK, HEAD_DIM], F32, tag="turned", bufs=4)
+                    for hh in range(HEADS_PER_CHUNK):
+                        nc.tensor.transpose(
+                            k_bank[:, hh, :], kT[:, hh, jj * P : (jj + 1) * P], identity[:]
+                        )
+                    nc.vector.tensor_tensor(
+                        out=products[:, :, r],
+                        in0=k_bank[:].unsqueeze(1).to_broadcast(shape),
+                        in1=tables[:, j].unsqueeze(2).to_broadcast(shape),
+                        op=MULT,
+                    )
+                nc.gpsimd.tensor_tensor(
+                    out=products[:, 0, :, :, :HALF_DIM],
+                    in0=products[:, 0, :, :, :HALF_DIM],
+                    in1=products[:, 1, :, :, HALF_DIM:],
+                    op=SUBTRACT,
+                )
+                nc.gpsimd.tensor_tensor(
+                    out=products[:, 0, :, :, HALF_DIM:],
+                    in0=products[:, 0, :, :, HALF_DIM:],
+                    in1=products[:, 1, :, :, :HALF_DIM],
+                    op=ADD,
+                )
+                nc.sync.dma_start(
+                    out=out_0[first * P : (first + 2) * P, heads, :].rearrange(
+                        "(r p) h d -> p r h d", p=P
+                    ),
+                    in_=products[:, 0],
+                )
+
+        def values(half, q):
+            heads = slice(q * HEADS_PER_CHUNK, (q + 1) * HEADS_PER_CHUNK)
+            cols = slice(q * BANK, (q + 1) * BANK)
+            for first in range(half * TILES_PER_HALF, (half + 1) * TILES_PER_HALF, 2):
+                v_rows = results.tile([P, 2, BANK], F32, tag="v_rows")
+                for r in range(2):
+                    pos = slice((first + r) * P, (first + r + 1) * P)
+                    v_bank = banks.tile([P, BANK], F32, tag="for_vector")
+                    nc.tensor.matmul_mx(
+                        out=v_bank[:],
+                        lhsT=c_codes[:, pos].bitcast(FP8X4),
+                        lhsT_scale=c_scales[:, pos],
+                        rhs=wv_codes[:, cols].bitcast(FP8X4),
+                        rhs_scale=wv_scales[:, cols],
+                        start=True,
+                        stop=True,
+                    )
+                    nc.vector.tensor_tensor(
+                        out=v_rows[:, r, :], in0=v_bank[:], in1=bv_all[:, cols], op=ADD
+                    )
+                nc.sync.dma_start(
+                    out=out_1[first * P : (first + 2) * P, heads, :].rearrange(
+                        "(r p) h d -> p r (h d)", p=P
+                    ),
+                    in_=v_rows[:],
+                )
+
+        for g in range(D_PASSES):
+            quantise_512_rows(
+                nc, banks, stage, identity, shared_copies,
+                wkv_words[:, :, g * WORDS : (g + 1) * WORDS], wkv_codes[:, g, :], wkv_scales[:, g, :],
+            )
+
+        def prepare(half, q):
+            if q == 0:
+                quantise_x_half(half)
+                compress_half(half)
+            if half == 0:
+                quantise_up_weight(q, wk_words, wk_codes, wk_scales)
+                quantise_up_weight(q, wv_words, wv_codes, wv_scales)
+            return project_keys(half, q)
+
+        units = [(half, q) for half in range(S_HALVES) for q in range(E_CHUNKS)]
+        kT_next = prepare(*units[0])
+        for n, (half, q) in enumerate(units):
+            kT_now = kT_next
+            if n + 1 < len(units):
+                kT_next = prepare(*units[n + 1])
+            values(half, q)
+            rotate_keys(half, q, kT_now)

@@ -24,32 +24,35 @@ E = HEADS * HEAD_DIM
 HALF_DIM = HEAD_DIM // 2
 S_TILES = S // P
 S_HALVES = S // BANK
-TILES_PER_HALF = BANK // P
+TILES = BANK // P
 D_PASSES = D // K_PASS
-E_CHUNKS = E // BANK
-HEADS_PER_CHUNK = BANK // HEAD_DIM
+CHUNKS = E // BANK
+CHUNK_HEADS = BANK // HEAD_DIM
 
 FLOPS = 2 * S * D * CKV + 2 * 2 * S * CKV * E
 
 
-def quantise_512_rows(nc, banks, stage, identity, copies, raw_words, codes, scales):
+def quantise_rows(nc, banks, stage, identity, copies, raw_words, codes, scales):
+    row_tiles = raw_words.shape[1]
     grouped = stage.tile([P, 4 * P, PACK], BF16, tag="grouped", align_bytes=64)
     grouped_words = grouped[:].bitcast(F32)
-    for pair in range(2):
+    for first in range(0, row_tiles, 2):
         bank = banks.tile([P, 2, 2, P], F32, tag="turned", bufs=4)
         for r in range(2):
             for u in range(2):
                 nc.tensor.transpose(
-                    bank[:, r, u, :], raw_words[:, 2 * pair + r, u * P : (u + 1) * P], identity[:]
+                    bank[:, r, u, :], raw_words[:, first + r, u * P : (u + 1) * P], identity[:]
                 )
-        copies[pair](
-            out=grouped_words[:, 2 * pair * P : 2 * (pair + 1) * P, :].rearrange(
+        copies[first // 2](
+            out=grouped_words[:, first * P : (first + 2) * P, :].rearrange(
                 "p (r row) u -> p r row u", r=2
             ),
             in_=bank[:].rearrange("p r u row -> p r row u"),
         )
     nc.vector.quantize_mx(
-        out=codes.bitcast(FP8X4), scales=scales, in_=grouped[:].rearrange("p row t -> p (row t)")
+        out=codes.bitcast(FP8X4),
+        scales=scales,
+        in_=grouped[:, : row_tiles * P, :].rearrange("p row t -> p (row t)"),
     )
 
 
@@ -60,9 +63,9 @@ def tile_selfattention_pa_kernel(
     with ExitStack() as pools:
         keep = pools.enter_context(tc.tile_pool(name="keep", bufs=1))
         stage = pools.enter_context(tc.tile_pool(name="stage", bufs=4))
-        work = pools.enter_context(tc.tile_pool(name="work", bufs=2))
         results = pools.enter_context(tc.tile_pool(name="results", bufs=4))
         banks = pools.enter_context(tc.psum_pool(name="banks", bufs=2))
+        pools.enter_context(tc.manual_schedule())
 
         identity = keep.tile([P, P], F32)
         make_identity(nc, identity[:])
@@ -71,9 +74,9 @@ def tile_selfattention_pa_kernel(
         wkv_rows = wkv_down.rearrange("(u p e) d -> p u e d", u=2, e=2)
         for u in range(2):
             nc.sync.dma_start(out=wkv_raw[:, 2 * u : 2 * u + 2, :], in_=wkv_rows[:, u])
-        bkv = keep.tile([P, PACK], BF16)
+        bkv_bf16 = keep.tile([P, PACK], BF16)
         nc.sync.dma_start(
-            out=bkv[:].rearrange("p (u e) -> p u e", u=2),
+            out=bkv_bf16[:].rearrange("p (u e) -> p u e", u=2),
             in_=bkv_down.rearrange("(u p e) -> p u e", u=2, e=2),
         )
 
@@ -85,11 +88,11 @@ def tile_selfattention_pa_kernel(
         wv_rows = wv_up.rearrange("(h p) c -> p h c", p=P)
 
         def load_x_half(half):
-            for j in range(half * TILES_PER_HALF, (half + 1) * TILES_PER_HALF, 2):
+            for j in range(half * TILES, (half + 1) * TILES, 2):
                 nc.sync.dma_start(out=x_raw[:, j : j + 2, :], in_=x_rows[:, j : j + 2, :])
 
         def load_up_weights(q):
-            heads = slice(q * HEADS_PER_CHUNK, (q + 1) * HEADS_PER_CHUNK)
+            heads = slice(q * CHUNK_HEADS, (q + 1) * CHUNK_HEADS)
             nc.sync.dma_start(out=wk_raw[:, heads, :], in_=wk_rows[:, heads, :])
             nc.sync.dma_start(out=wv_raw[:, heads, :], in_=wv_rows[:, heads, :])
 
@@ -99,19 +102,16 @@ def tile_selfattention_pa_kernel(
         with nc.allow_non_contiguous_dma(reason="a 4 KiB bias, one element to a partition"):
             nc.sync.dma_start(out=bk_bf16[:], in_=bk_up.rearrange("(h d) -> d h", d=HEAD_DIM))
         tables = keep.tile([P, S_TILES, 2, HEAD_DIM], BF16)
-        cos_rows = rope_cos.rearrange("(j p) d -> p j d", p=P)
-        sin_rows = rope_sin.rearrange("(j p) d -> p j d", p=P)
-        nc.sync.dma_start(out=tables[:, :, 0, :], in_=cos_rows)
-        nc.sync.dma_start(out=tables[:, :, 1, :HALF_DIM], in_=sin_rows[:, :, HALF_DIM:])
-        nc.sync.dma_start(out=tables[:, :, 1, HALF_DIM:], in_=sin_rows[:, :, :HALF_DIM])
+        sin_raw = keep.tile([P, S_TILES, HEAD_DIM], BF16)
+        nc.sync.dma_start(out=tables[:, :, 0, :], in_=rope_cos.rearrange("(j p) d -> p j d", p=P))
+        nc.sync.dma_start(out=sin_raw[:], in_=rope_sin.rearrange("(j p) d -> p j d", p=P))
+        nc.gpsimd.tensor_copy(out=tables[:, :, 1, :HALF_DIM], in_=sin_raw[:, :, HALF_DIM:])
+        nc.gpsimd.tensor_copy(out=tables[:, :, 1, HALF_DIM:], in_=sin_raw[:, :, :HALF_DIM])
         bv_all = keep.tile([P, E], BF16)
         nc.sync.dma_start(out=bv_all[:], in_=bv_up.partition_broadcast(P))
-        for q in range(1, E_CHUNKS):
+        for q in range(1, CHUNKS):
             load_up_weights(q)
         load_x_half(1)
-
-        bk = keep.tile([P, HEADS], F32)
-        nc.vector.tensor_copy(out=bk[:], in_=bk_bf16[:])
 
         wkv_codes = keep.tile([P, D_PASSES, CKV], U32, align_bytes=64)
         wkv_scales = keep.tile([P, D_PASSES, CKV], U8, align_bytes=64)
@@ -129,164 +129,180 @@ def tile_selfattention_pa_kernel(
         wk_words = wk_raw[:].bitcast(F32)
         wv_words = wv_raw[:].bitcast(F32)
 
-        shared_copies = (nc.scalar.copy, nc.vector.tensor_copy)
-        scalar_copies = (nc.scalar.copy, nc.scalar.copy)
-
-        def quantise_x_half(half):
-            tiles = slice(half * TILES_PER_HALF, (half + 1) * TILES_PER_HALF)
-            cols = slice(half * BANK, (half + 1) * BANK)
-            copies = shared_copies if half == 0 else scalar_copies
-            for g in range(D_PASSES):
-                quantise_512_rows(
-                    nc, banks, stage, identity, copies,
-                    x_words[:, tiles, g * WORDS : (g + 1) * WORDS],
-                    x_codes[:, g, cols], x_scales[:, g, cols],
-                )
-
-        def quantise_up_weight(q, words, codes, scales):
-            heads = slice(q * HEADS_PER_CHUNK, (q + 1) * HEADS_PER_CHUNK)
-            cols = slice(q * BANK, (q + 1) * BANK)
-            quantise_512_rows(
-                nc, banks, stage, identity, scalar_copies,
-                words[:, heads, :], codes[:, cols], scales[:, cols],
-            )
-
-        def compress_half(half):
-            c_grouped = stage.tile([P, BANK, PACK], BF16, tag="grouped", align_bytes=64)
-            for jj in range(TILES_PER_HALF):
-                pos = slice((half * TILES_PER_HALF + jj) * P, (half * TILES_PER_HALF + jj + 1) * P)
-                c_bank = banks.tile([P, PACK, P], F32, tag="for_vector")
-                for t in range(PACK):
-                    rows = slice(t * P, (t + 1) * P)
-                    for g in range(D_PASSES):
-                        nc.tensor.matmul_mx(
-                            out=c_bank[:, t, :],
-                            lhsT=wkv_codes[:, g, rows].bitcast(FP8X4),
-                            lhsT_scale=wkv_scales[:, g, rows],
-                            rhs=x_codes[:, g, pos].bitcast(FP8X4),
-                            rhs_scale=x_scales[:, g, pos],
-                            start=(g == 0),
-                            stop=(g == D_PASSES - 1),
-                        )
-                nc.vector.tensor_tensor(
-                    out=c_grouped[:, jj * P : (jj + 1) * P, :],
-                    in0=c_bank[:].rearrange("p t s -> p s t"),
-                    in1=bkv[:].unsqueeze(1).to_broadcast([P, P, PACK]),
-                    op=ADD,
-                )
-            cols = slice(half * BANK, (half + 1) * BANK)
-            nc.vector.quantize_mx(
-                out=c_codes[:, cols].bitcast(FP8X4),
-                scales=c_scales[:, cols],
-                in_=c_grouped[:].rearrange("p s t -> p (s t)"),
-            )
-
-        def project_keys(half, q):
-            pos = slice(half * BANK, (half + 1) * BANK)
-            kT = work.tile([P, HEADS_PER_CHUNK, BANK], F32, tag="kT")
-            for hh in range(HEADS_PER_CHUNK):
-                h = q * HEADS_PER_CHUNK + hh
-                cols = slice(h * HEAD_DIM, (h + 1) * HEAD_DIM)
-                kT_bank = banks.tile([P, BANK], F32, tag="for_scalar")
-                nc.tensor.matmul_mx(
-                    out=kT_bank[:],
-                    lhsT=wk_codes[:, cols].bitcast(FP8X4),
-                    lhsT_scale=wk_scales[:, cols],
-                    rhs=c_codes[:, pos].bitcast(FP8X4),
-                    rhs_scale=c_scales[:, pos],
-                    start=True,
-                    stop=True,
-                )
-                nc.scalar.activation(
-                    out=kT[:, hh, :], in_=kT_bank[:], func=IDENTITY, bias=bk[:, h : h + 1], scale=1.0
-                )
-            return kT
-
-        def rotate_keys(half, q, kT):
-            heads = slice(q * HEADS_PER_CHUNK, (q + 1) * HEADS_PER_CHUNK)
-            shape = [P, 2, HEADS_PER_CHUNK, HEAD_DIM]
-            for first in range(half * TILES_PER_HALF, (half + 1) * TILES_PER_HALF, 2):
-                products = results.tile([P, 2, 2, HEADS_PER_CHUNK, HEAD_DIM], F32, tag="products")
-                for r in range(2):
-                    j = first + r
-                    jj = j - half * TILES_PER_HALF
-                    k_bank = banks.tile([P, HEADS_PER_CHUNK, HEAD_DIM], F32, tag="turned", bufs=4)
-                    for hh in range(HEADS_PER_CHUNK):
-                        nc.tensor.transpose(
-                            k_bank[:, hh, :], kT[:, hh, jj * P : (jj + 1) * P], identity[:]
-                        )
-                    nc.vector.tensor_tensor(
-                        out=products[:, :, r],
-                        in0=k_bank[:].unsqueeze(1).to_broadcast(shape),
-                        in1=tables[:, j].unsqueeze(2).to_broadcast(shape),
-                        op=MULT,
-                    )
-                nc.gpsimd.tensor_tensor(
-                    out=products[:, 0, :, :, :HALF_DIM],
-                    in0=products[:, 0, :, :, :HALF_DIM],
-                    in1=products[:, 1, :, :, HALF_DIM:],
-                    op=SUBTRACT,
-                )
-                nc.gpsimd.tensor_tensor(
-                    out=products[:, 0, :, :, HALF_DIM:],
-                    in0=products[:, 0, :, :, HALF_DIM:],
-                    in1=products[:, 1, :, :, :HALF_DIM],
-                    op=ADD,
-                )
-                nc.sync.dma_start(
-                    out=out_0[first * P : (first + 2) * P, heads, :].rearrange(
-                        "(r p) h d -> p r h d", p=P
-                    ),
-                    in_=products[:, 0],
-                )
-
-        def values(half, q):
-            heads = slice(q * HEADS_PER_CHUNK, (q + 1) * HEADS_PER_CHUNK)
-            cols = slice(q * BANK, (q + 1) * BANK)
-            for first in range(half * TILES_PER_HALF, (half + 1) * TILES_PER_HALF, 2):
-                v_rows = results.tile([P, 2, BANK], F32, tag="v_rows")
-                for r in range(2):
-                    pos = slice((first + r) * P, (first + r + 1) * P)
-                    v_bank = banks.tile([P, BANK], F32, tag="for_vector")
-                    nc.tensor.matmul_mx(
-                        out=v_bank[:],
-                        lhsT=c_codes[:, pos].bitcast(FP8X4),
-                        lhsT_scale=c_scales[:, pos],
-                        rhs=wv_codes[:, cols].bitcast(FP8X4),
-                        rhs_scale=wv_scales[:, cols],
-                        start=True,
-                        stop=True,
-                    )
-                    nc.vector.tensor_tensor(
-                        out=v_rows[:, r, :], in0=v_bank[:], in1=bv_all[:, cols], op=ADD
-                    )
-                nc.sync.dma_start(
-                    out=out_1[first * P : (first + 2) * P, heads, :].rearrange(
-                        "(r p) h d -> p r (h d)", p=P
-                    ),
-                    in_=v_rows[:],
-                )
-
-        for g in range(D_PASSES):
-            quantise_512_rows(
-                nc, banks, stage, identity, shared_copies,
+        def quantise_wkv(g, copies):
+            quantise_rows(
+                nc, banks, stage, identity, copies,
                 wkv_words[:, :, g * WORDS : (g + 1) * WORDS], wkv_codes[:, g, :], wkv_scales[:, g, :],
             )
 
-        def prepare(half, q):
-            if q == 0:
-                quantise_x_half(half)
-                compress_half(half)
-            if half == 0:
-                quantise_up_weight(q, wk_words, wk_codes, wk_scales)
-                quantise_up_weight(q, wv_words, wv_codes, wv_scales)
-            return project_keys(half, q)
+        def quantise_x(first_tile, tiles, g, copies):
+            cols = slice(first_tile * P, (first_tile + tiles) * P)
+            quantise_rows(
+                nc, banks, stage, identity, copies,
+                x_words[:, first_tile : first_tile + tiles, g * WORDS : (g + 1) * WORDS],
+                x_codes[:, g, cols], x_scales[:, g, cols],
+            )
 
-        units = [(half, q) for half in range(S_HALVES) for q in range(E_CHUNKS)]
-        kT_next = prepare(*units[0])
-        for n, (half, q) in enumerate(units):
-            kT_now = kT_next
-            if n + 1 < len(units):
-                kT_next = prepare(*units[n + 1])
-            values(half, q)
-            rotate_keys(half, q, kT_now)
+        def quantise_wk(q, copies):
+            cols = slice(q * BANK, (q + 1) * BANK)
+            quantise_rows(
+                nc, banks, stage, identity, copies,
+                wk_words[:, q * CHUNK_HEADS : (q + 1) * CHUNK_HEADS, :],
+                wk_codes[:, cols], wk_scales[:, cols],
+            )
+
+        def quantise_wv(q, copies):
+            cols = slice(q * BANK, (q + 1) * BANK)
+            quantise_rows(
+                nc, banks, stage, identity, copies,
+                wv_words[:, q * CHUNK_HEADS : (q + 1) * CHUNK_HEADS, :],
+                wv_codes[:, cols], wv_scales[:, cols],
+            )
+
+        bkv = keep.tile([P, PACK], F32)
+        bk = keep.tile([P, HEADS], F32)
+        c_rows = keep.tile([P, S_HALVES, PACK, BANK], BF16)
+
+        def compress(half, t):
+            pos = slice(half * BANK, (half + 1) * BANK)
+            rows = slice(t * P, (t + 1) * P)
+            c_bank = banks.tile([P, BANK], F32, tag="for_scalar")
+            for g in range(D_PASSES):
+                nc.tensor.matmul_mx(
+                    out=c_bank[:],
+                    lhsT=wkv_codes[:, g, rows].bitcast(FP8X4),
+                    lhsT_scale=wkv_scales[:, g, rows],
+                    rhs=x_codes[:, g, pos].bitcast(FP8X4),
+                    rhs_scale=x_scales[:, g, pos],
+                    start=(g == 0),
+                    stop=(g == D_PASSES - 1),
+                )
+            nc.scalar.activation(
+                out=c_rows[:, half, t, :], in_=c_bank[:], func=IDENTITY, bias=bkv[:, t : t + 1],
+                scale=1.0,
+            )
+
+        def quantise_c(half):
+            pos = slice(half * BANK, (half + 1) * BANK)
+            c_grouped = stage.tile([P, BANK, PACK], BF16, tag="grouped", align_bytes=64)
+            nc.vector.tensor_copy(out=c_grouped[:], in_=c_rows[:, half].rearrange("p t s -> p s t"))
+            nc.vector.quantize_mx(
+                out=c_codes[:, pos].bitcast(FP8X4),
+                scales=c_scales[:, pos],
+                in_=c_grouped[:].rearrange("p s t -> p (s t)"),
+            )
+
+        def project_key_head(half, h):
+            pos = slice(half * BANK, (half + 1) * BANK)
+            cols = slice(h * HEAD_DIM, (h + 1) * HEAD_DIM)
+            kT_bank = banks.tile([P, BANK], F32, tag="for_scalar")
+            nc.tensor.matmul_mx(
+                out=kT_bank[:],
+                lhsT=wk_codes[:, cols].bitcast(FP8X4),
+                lhsT_scale=wk_scales[:, cols],
+                rhs=c_codes[:, pos].bitcast(FP8X4),
+                rhs_scale=c_scales[:, pos],
+                start=True,
+                stop=True,
+            )
+            kT = stage.tile([P, BANK], F32, tag="kT")
+            nc.scalar.activation(
+                out=kT[:], in_=kT_bank[:], func=IDENTITY, bias=bk[:, h : h + 1], scale=1.0
+            )
+            return kT
+
+        def project_values(j, q, v_rows):
+            pos = slice(j * P, (j + 1) * P)
+            cols = slice(q * BANK, (q + 1) * BANK)
+            v_bank = banks.tile([P, BANK], F32, tag="for_vector")
+            nc.tensor.matmul_mx(
+                out=v_bank[:],
+                lhsT=c_codes[:, pos].bitcast(FP8X4),
+                lhsT_scale=c_scales[:, pos],
+                rhs=wv_codes[:, cols].bitcast(FP8X4),
+                rhs_scale=wv_scales[:, cols],
+                start=True,
+                stop=True,
+            )
+            nc.vector.tensor_tensor(out=v_rows, in0=v_bank[:], in1=bv_all[:, cols], op=ADD)
+
+        def rope_products(half, kT, products):
+            k_bank = banks.tile([P, TILES, HEAD_DIM], F32, tag="turned", bufs=4)
+            for jj in range(TILES):
+                nc.tensor.transpose(k_bank[:, jj, :], kT[:, jj * P : (jj + 1) * P], identity[:])
+            nc.vector.tensor_tensor(
+                out=products,
+                in0=k_bank[:].unsqueeze(1).to_broadcast([P, 2, TILES, HEAD_DIM]),
+                in1=tables[:, half * TILES : (half + 1) * TILES].rearrange("p j c d -> p c j d"),
+                op=MULT,
+            )
+
+        def rope_sums(products):
+            nc.gpsimd.tensor_tensor(
+                out=products[:, 0, :, :, :HALF_DIM],
+                in0=products[:, 0, :, :, :HALF_DIM],
+                in1=products[:, 1, :, :, HALF_DIM:],
+                op=SUBTRACT,
+            )
+            nc.gpsimd.tensor_tensor(
+                out=products[:, 0, :, :, HALF_DIM:],
+                in0=products[:, 0, :, :, HALF_DIM:],
+                in1=products[:, 1, :, :, :HALF_DIM],
+                op=ADD,
+            )
+
+        nc.vector.tensor_copy(out=bkv[:], in_=bkv_bf16[:])
+        scalar_only = (nc.scalar.copy, nc.scalar.copy)
+        shared = (nc.scalar.copy, nc.vector.tensor_copy)
+        for g in range(D_PASSES):
+            quantise_wkv(g, shared)
+        for first_tile in range(0, TILES, 2):
+            for g in range(D_PASSES):
+                quantise_x(first_tile, 2, g, scalar_only)
+        quantise_wv(0, shared)
+        quantise_wk(0, shared)
+        nc.vector.tensor_copy(out=bk[:], in_=bk_bf16[:])
+        for t in range(PACK):
+            compress(0, t)
+        quantise_c(0)
+
+        later = []
+        for q in range(1, CHUNKS):
+            later.append((quantise_wk, (q, scalar_only)))
+            later.append((quantise_wv, (q, scalar_only)))
+        for g in range(D_PASSES):
+            later.append((quantise_x, (TILES, TILES, g, scalar_only)))
+        for t in range(PACK):
+            later.append((compress, (1, t)))
+        later.append((quantise_c, (1,)))
+
+        steps = [(half, h) for half in range(S_HALVES) for h in range(HEADS)]
+        kT_next = project_key_head(*steps[0])
+        for step, (half, h) in enumerate(steps):
+            q, i = divmod(h, CHUNK_HEADS)
+            j = half * TILES + i
+            if h % 2 == 0:
+                products = results.tile([P, 2, TILES, 2, HEAD_DIM], F32, tag="products")
+                v_rows = results.tile([P, 2, BANK], F32, tag="v_rows")
+            kT = kT_next
+            if step + 1 < len(steps):
+                kT_next = project_key_head(*steps[step + 1])
+            project_values(j, q, v_rows[:, h % 2, :])
+            rope_products(half, kT, products[:, :, :, h % 2, :])
+            if step < len(later):
+                piece, arguments = later[step]
+                piece(*arguments)
+            if h % 2 == 1:
+                rope_sums(products)
+                nc.sync.dma_start(
+                    out=out_1[
+                        (j - 1) * P : (j + 1) * P, q * CHUNK_HEADS : (q + 1) * CHUNK_HEADS, :
+                    ].rearrange("(r p) h d -> p r (h d)", p=P),
+                    in_=v_rows[:],
+                )
+                nc.sync.dma_start(
+                    out=out_0[half * BANK : (half + 1) * BANK, h - 1 : h + 1, :].rearrange(
+                        "(j p) h d -> p j h d", p=P
+                    ),
+                    in_=products[:, 0],
+                )

@@ -69,6 +69,11 @@ def tile_selfattention_pa_kernel(
 
         identity = keep.tile([P, P], F32)
         make_identity(nc, identity[:])
+        identity_bf16 = keep.tile([P, P], BF16)
+        make_identity(nc, identity_bf16[:])
+        exchange = keep.tile([P, P], F32)
+        nc.gpsimd.tensor_copy(out=exchange[:, :HALF_DIM], in_=identity[:, HALF_DIM:])
+        nc.gpsimd.tensor_copy(out=exchange[:, HALF_DIM:], in_=identity[:, :HALF_DIM])
 
         wkv_raw = keep.tile([P, PACK, D], BF16)
         wkv_rows = wkv_down.rearrange("(u p e) d -> p u e d", u=2, e=2)
@@ -97,16 +102,19 @@ def tile_selfattention_pa_kernel(
             nc.sync.dma_start(out=wv_raw[:, heads, :], in_=wv_rows[:, heads, :])
 
         load_x_half(0)
-        load_up_weights(0)
         bk_bf16 = keep.tile([P, HEADS], BF16)
         with nc.allow_non_contiguous_dma(reason="a 4 KiB bias, one element to a partition"):
             nc.sync.dma_start(out=bk_bf16[:], in_=bk_up.rearrange("(h d) -> d h", d=HEAD_DIM))
-        tables = keep.tile([P, S_TILES, 2, HEAD_DIM], BF16)
+        table_rows = keep.tile([P, S_TILES, 2, HEAD_DIM], BF16)
         sin_raw = keep.tile([P, S_TILES, HEAD_DIM], BF16)
-        nc.sync.dma_start(out=tables[:, :, 0, :], in_=rope_cos.rearrange("(j p) d -> p j d", p=P))
+        nc.sync.dma_start(out=table_rows[:, :, 0, :], in_=rope_cos.rearrange("(j p) d -> p j d", p=P))
         nc.sync.dma_start(out=sin_raw[:], in_=rope_sin.rearrange("(j p) d -> p j d", p=P))
-        nc.gpsimd.tensor_copy(out=tables[:, :, 1, :HALF_DIM], in_=sin_raw[:, :, HALF_DIM:])
-        nc.gpsimd.tensor_copy(out=tables[:, :, 1, HALF_DIM:], in_=sin_raw[:, :, :HALF_DIM])
+        nc.gpsimd.tensor_copy(out=table_rows[:, :, 1, :HALF_DIM], in_=sin_raw[:, :, HALF_DIM:])
+        nc.gpsimd.tensor_scalar(
+            out=table_rows[:, :, 1, HALF_DIM:], in0=sin_raw[:, :, :HALF_DIM],
+            scalar1=-1.0, scalar2=0.0, op0=MULT, op1=ADD,
+        )
+        load_up_weights(0)
         bv_all = keep.tile([P, E], BF16)
         nc.sync.dma_start(out=bv_all[:], in_=bv_up.partition_broadcast(P))
         for q in range(1, CHUNKS):
@@ -192,10 +200,21 @@ def tile_selfattention_pa_kernel(
                 in_=c_grouped[:].rearrange("p s t -> p (s t)"),
             )
 
+        tables = keep.tile([P, 2, S], BF16)
+
+        def transpose_tables():
+            for plane in range(2):
+                table_bank = banks.tile([P, S], BF16, tag="turned", bufs=4)
+                for j in range(S_TILES):
+                    nc.tensor.transpose(
+                        table_bank[:, j * P : (j + 1) * P], table_rows[:, j, plane, :], identity_bf16[:]
+                    )
+                nc.scalar.copy(out=tables[:, plane, :], in_=table_bank[:])
+
         def project_key_head(half, h):
             pos = slice(half * BANK, (half + 1) * BANK)
             cols = slice(h * HEAD_DIM, (h + 1) * HEAD_DIM)
-            kT_bank = banks.tile([P, BANK], F32, tag="for_scalar")
+            kT_bank = banks.tile([P, BANK], F32, tag="for_vector")
             nc.tensor.matmul_mx(
                 out=kT_bank[:],
                 lhsT=wk_codes[:, cols].bitcast(FP8X4),
@@ -205,16 +224,38 @@ def tile_selfattention_pa_kernel(
                 start=True,
                 stop=True,
             )
-            kT = stage.tile([P, BANK], F32, tag="kT")
-            nc.scalar.activation(
-                out=kT[:], in_=kT_bank[:], func=IDENTITY, bias=bk[:, h : h + 1], scale=1.0
+            return kT_bank
+
+        def rope_products(half, h, kT_bank):
+            products = stage.tile([P, 2, BANK], F32, tag="products")
+            nc.vector.scalar_tensor_tensor(
+                out=products[:],
+                in0=kT_bank[:].unsqueeze(1).to_broadcast([P, 2, BANK]),
+                scalar=bk[:, h : h + 1],
+                in1=tables[:, :, half * BANK : (half + 1) * BANK],
+                op0=ADD,
+                op1=MULT,
             )
-            return kT
+            return products
+
+        def rope_sums(products, k_rows):
+            k_bank = banks.tile([P, TILES, HEAD_DIM], F32, tag="turned", bufs=4)
+            for jj in range(TILES):
+                pos = slice(jj * P, (jj + 1) * P)
+                nc.tensor.matmul(
+                    out=k_bank[:, jj, :], lhsT=products[:, 0, pos], rhs=identity[:],
+                    is_transpose=True, start=True, stop=False,
+                )
+                nc.tensor.matmul(
+                    out=k_bank[:, jj, :], lhsT=products[:, 1, pos], rhs=exchange[:],
+                    is_transpose=True, start=False, stop=True,
+                )
+            nc.scalar.copy(out=k_rows, in_=k_bank[:])
 
         def project_values(j, q, v_rows):
             pos = slice(j * P, (j + 1) * P)
             cols = slice(q * BANK, (q + 1) * BANK)
-            v_bank = banks.tile([P, BANK], F32, tag="for_vector")
+            v_bank = banks.tile([P, BANK], F32, tag="for_scalar")
             nc.tensor.matmul_mx(
                 out=v_bank[:],
                 lhsT=c_codes[:, pos].bitcast(FP8X4),
@@ -224,32 +265,8 @@ def tile_selfattention_pa_kernel(
                 start=True,
                 stop=True,
             )
-            nc.vector.tensor_tensor(out=v_rows, in0=v_bank[:], in1=bv_all[:, cols], op=ADD)
-
-        def rope_products(half, kT, products):
-            k_bank = banks.tile([P, TILES, HEAD_DIM], F32, tag="turned", bufs=4)
-            for jj in range(TILES):
-                nc.tensor.transpose(k_bank[:, jj, :], kT[:, jj * P : (jj + 1) * P], identity[:])
-            nc.vector.tensor_tensor(
-                out=products,
-                in0=k_bank[:].unsqueeze(1).to_broadcast([P, 2, TILES, HEAD_DIM]),
-                in1=tables[:, half * TILES : (half + 1) * TILES].rearrange("p j c d -> p c j d"),
-                op=MULT,
-            )
-
-        def rope_sums(products):
-            nc.gpsimd.tensor_tensor(
-                out=products[:, 0, :, :, :HALF_DIM],
-                in0=products[:, 0, :, :, :HALF_DIM],
-                in1=products[:, 1, :, :, HALF_DIM:],
-                op=SUBTRACT,
-            )
-            nc.gpsimd.tensor_tensor(
-                out=products[:, 0, :, :, HALF_DIM:],
-                in0=products[:, 0, :, :, HALF_DIM:],
-                in1=products[:, 1, :, :, :HALF_DIM],
-                op=ADD,
-            )
+            nc.scalar.copy(out=v_rows, in_=v_bank[:])
+            nc.gpsimd.tensor_tensor(out=v_rows, in0=v_rows, in1=bv_all[:, cols], op=ADD)
 
         nc.vector.tensor_copy(out=bkv[:], in_=bkv_bf16[:])
         scalar_only = (nc.scalar.copy, nc.scalar.copy)
@@ -259,50 +276,58 @@ def tile_selfattention_pa_kernel(
         for first_tile in range(0, TILES, 2):
             for g in range(D_PASSES):
                 quantise_x(first_tile, 2, g, scalar_only)
+        for t in range(PACK):
+            compress(0, t)
         quantise_wv(0, shared)
         quantise_wk(0, shared)
         nc.vector.tensor_copy(out=bk[:], in_=bk_bf16[:])
-        for t in range(PACK):
-            compress(0, t)
+        transpose_tables()
         quantise_c(0)
 
         later = []
         for q in range(1, CHUNKS):
-            later.append((quantise_wk, (q, scalar_only)))
-            later.append((quantise_wv, (q, scalar_only)))
+            later.append((quantise_wk, (q, shared)))
+            later.append((quantise_wv, (q, shared)))
         for g in range(D_PASSES):
-            later.append((quantise_x, (TILES, TILES, g, scalar_only)))
+            later.append((quantise_x, (TILES, TILES, g, shared)))
         for t in range(PACK):
             later.append((compress, (1, t)))
         later.append((quantise_c, (1,)))
 
+        def finish_head(half, h, products, k_rows):
+            rope_sums(products, k_rows[:, :, h % 2, :])
+            if h % 2 == 1:
+                nc.sync.dma_start(
+                    out=out_0[half * BANK : (half + 1) * BANK, h - 1 : h + 1, :].rearrange(
+                        "(j p) h d -> p j h d", p=P
+                    ),
+                    in_=k_rows[:],
+                )
+
         steps = [(half, h) for half in range(S_HALVES) for h in range(HEADS)]
-        kT_next = project_key_head(*steps[0])
+        kT_bank_next = project_key_head(*steps[0])
+        unfinished = None
         for step, (half, h) in enumerate(steps):
             q, i = divmod(h, CHUNK_HEADS)
             j = half * TILES + i
             if h % 2 == 0:
-                products = results.tile([P, 2, TILES, 2, HEAD_DIM], F32, tag="products")
+                k_rows = results.tile([P, TILES, 2, HEAD_DIM], F32, tag="k_rows")
                 v_rows = results.tile([P, 2, BANK], F32, tag="v_rows")
-            kT = kT_next
+            kT_bank = kT_bank_next
             if step + 1 < len(steps):
-                kT_next = project_key_head(*steps[step + 1])
+                kT_bank_next = project_key_head(*steps[step + 1])
             project_values(j, q, v_rows[:, h % 2, :])
-            rope_products(half, kT, products[:, :, :, h % 2, :])
+            if unfinished is not None:
+                finish_head(*unfinished)
+            unfinished = (half, h, rope_products(half, h, kT_bank), k_rows)
             if step < len(later):
                 piece, arguments = later[step]
                 piece(*arguments)
             if h % 2 == 1:
-                rope_sums(products)
                 nc.sync.dma_start(
                     out=out_1[
                         (j - 1) * P : (j + 1) * P, q * CHUNK_HEADS : (q + 1) * CHUNK_HEADS, :
                     ].rearrange("(r p) h d -> p r (h d)", p=P),
                     in_=v_rows[:],
                 )
-                nc.sync.dma_start(
-                    out=out_0[half * BANK : (half + 1) * BANK, h - 1 : h + 1, :].rearrange(
-                        "(j p) h d -> p j h d", p=P
-                    ),
-                    in_=products[:, 0],
-                )
+        finish_head(*unfinished)

@@ -65,15 +65,9 @@ def tile_selfattention_pa_kernel(
         stage = pools.enter_context(tc.tile_pool(name="stage", bufs=4))
         results = pools.enter_context(tc.tile_pool(name="results", bufs=4))
         banks = pools.enter_context(tc.psum_pool(name="banks", bufs=2))
-        pools.enter_context(tc.manual_schedule())
 
         identity = keep.tile([P, P], F32)
         make_identity(nc, identity[:])
-        identity_bf16 = keep.tile([P, P], BF16)
-        make_identity(nc, identity_bf16[:])
-        exchange = keep.tile([P, P], F32)
-        nc.gpsimd.tensor_copy(out=exchange[:, :HALF_DIM], in_=identity[:, HALF_DIM:])
-        nc.gpsimd.tensor_copy(out=exchange[:, HALF_DIM:], in_=identity[:, :HALF_DIM])
 
         wkv_raw = keep.tile([P, PACK, D], BF16)
         wkv_rows = wkv_down.rearrange("(u p e) d -> p u e d", u=2, e=2)
@@ -102,19 +96,16 @@ def tile_selfattention_pa_kernel(
             nc.sync.dma_start(out=wv_raw[:, heads, :], in_=wv_rows[:, heads, :])
 
         load_x_half(0)
+        load_up_weights(0)
         bk_bf16 = keep.tile([P, HEADS], BF16)
         with nc.allow_non_contiguous_dma(reason="a 4 KiB bias, one element to a partition"):
             nc.sync.dma_start(out=bk_bf16[:], in_=bk_up.rearrange("(h d) -> d h", d=HEAD_DIM))
-        table_rows = keep.tile([P, S_TILES, 2, HEAD_DIM], BF16)
+        tables = keep.tile([P, S_TILES, 2, HEAD_DIM], BF16)
         sin_raw = keep.tile([P, S_TILES, HEAD_DIM], BF16)
-        nc.sync.dma_start(out=table_rows[:, :, 0, :], in_=rope_cos.rearrange("(j p) d -> p j d", p=P))
+        nc.sync.dma_start(out=tables[:, :, 0, :], in_=rope_cos.rearrange("(j p) d -> p j d", p=P))
         nc.sync.dma_start(out=sin_raw[:], in_=rope_sin.rearrange("(j p) d -> p j d", p=P))
-        nc.gpsimd.tensor_copy(out=table_rows[:, :, 1, :HALF_DIM], in_=sin_raw[:, :, HALF_DIM:])
-        nc.gpsimd.tensor_scalar(
-            out=table_rows[:, :, 1, HALF_DIM:], in0=sin_raw[:, :, :HALF_DIM],
-            scalar1=-1.0, scalar2=0.0, op0=MULT, op1=ADD,
-        )
-        load_up_weights(0)
+        nc.gpsimd.tensor_copy(out=tables[:, :, 1, :HALF_DIM], in_=sin_raw[:, :, HALF_DIM:])
+        nc.gpsimd.tensor_copy(out=tables[:, :, 1, HALF_DIM:], in_=sin_raw[:, :, :HALF_DIM])
         bv_all = keep.tile([P, E], BF16)
         nc.sync.dma_start(out=bv_all[:], in_=bv_up.partition_broadcast(P))
         for q in range(1, CHUNKS):
@@ -200,21 +191,10 @@ def tile_selfattention_pa_kernel(
                 in_=c_grouped[:].rearrange("p s t -> p (s t)"),
             )
 
-        tables = keep.tile([P, 2, S], BF16)
-
-        def transpose_tables():
-            for plane in range(2):
-                table_bank = banks.tile([P, S], BF16, tag="turned", bufs=4)
-                for j in range(S_TILES):
-                    nc.tensor.transpose(
-                        table_bank[:, j * P : (j + 1) * P], table_rows[:, j, plane, :], identity_bf16[:]
-                    )
-                nc.scalar.copy(out=tables[:, plane, :], in_=table_bank[:])
-
         def project_key_head(half, h):
             pos = slice(half * BANK, (half + 1) * BANK)
             cols = slice(h * HEAD_DIM, (h + 1) * HEAD_DIM)
-            kT_bank = banks.tile([P, BANK], F32, tag="for_vector")
+            kT_bank = banks.tile([P, BANK], F32, tag="for_scalar")
             nc.tensor.matmul_mx(
                 out=kT_bank[:],
                 lhsT=wk_codes[:, cols].bitcast(FP8X4),
@@ -224,38 +204,16 @@ def tile_selfattention_pa_kernel(
                 start=True,
                 stop=True,
             )
-            return kT_bank
-
-        def rope_products(half, h, kT_bank):
-            products = stage.tile([P, 2, BANK], F32, tag="products")
-            nc.vector.scalar_tensor_tensor(
-                out=products[:],
-                in0=kT_bank[:].unsqueeze(1).to_broadcast([P, 2, BANK]),
-                scalar=bk[:, h : h + 1],
-                in1=tables[:, :, half * BANK : (half + 1) * BANK],
-                op0=ADD,
-                op1=MULT,
+            kT = stage.tile([P, BANK], F32, tag="kT")
+            nc.scalar.activation(
+                out=kT[:], in_=kT_bank[:], func=IDENTITY, bias=bk[:, h : h + 1], scale=1.0
             )
-            return products
-
-        def rope_sums(products, k_rows):
-            k_bank = banks.tile([P, TILES, HEAD_DIM], F32, tag="turned", bufs=4)
-            for jj in range(TILES):
-                pos = slice(jj * P, (jj + 1) * P)
-                nc.tensor.matmul(
-                    out=k_bank[:, jj, :], lhsT=products[:, 0, pos], rhs=identity[:],
-                    is_transpose=True, start=True, stop=False,
-                )
-                nc.tensor.matmul(
-                    out=k_bank[:, jj, :], lhsT=products[:, 1, pos], rhs=exchange[:],
-                    is_transpose=True, start=False, stop=True,
-                )
-            nc.scalar.copy(out=k_rows, in_=k_bank[:])
+            return kT
 
         def project_values(j, q, v_rows):
             pos = slice(j * P, (j + 1) * P)
             cols = slice(q * BANK, (q + 1) * BANK)
-            v_bank = banks.tile([P, BANK], F32, tag="for_scalar")
+            v_bank = banks.tile([P, BANK], F32, tag="for_vector")
             nc.tensor.matmul_mx(
                 out=v_bank[:],
                 lhsT=c_codes[:, pos].bitcast(FP8X4),
@@ -265,8 +223,32 @@ def tile_selfattention_pa_kernel(
                 start=True,
                 stop=True,
             )
-            nc.scalar.copy(out=v_rows, in_=v_bank[:])
-            nc.gpsimd.tensor_tensor(out=v_rows, in0=v_rows, in1=bv_all[:, cols], op=ADD)
+            nc.vector.tensor_tensor(out=v_rows, in0=v_bank[:], in1=bv_all[:, cols], op=ADD)
+
+        def rope_products(half, kT, products):
+            k_bank = banks.tile([P, TILES, HEAD_DIM], F32, tag="turned", bufs=4)
+            for jj in range(TILES):
+                nc.tensor.transpose(k_bank[:, jj, :], kT[:, jj * P : (jj + 1) * P], identity[:])
+            nc.vector.tensor_tensor(
+                out=products,
+                in0=k_bank[:].unsqueeze(1).to_broadcast([P, 2, TILES, HEAD_DIM]),
+                in1=tables[:, half * TILES : (half + 1) * TILES].rearrange("p j c d -> p c j d"),
+                op=MULT,
+            )
+
+        def rope_sums(products):
+            nc.gpsimd.tensor_tensor(
+                out=products[:, 0, :, :, :HALF_DIM],
+                in0=products[:, 0, :, :, :HALF_DIM],
+                in1=products[:, 1, :, :, HALF_DIM:],
+                op=SUBTRACT,
+            )
+            nc.gpsimd.tensor_tensor(
+                out=products[:, 0, :, :, HALF_DIM:],
+                in0=products[:, 0, :, :, HALF_DIM:],
+                in1=products[:, 1, :, :, :HALF_DIM],
+                op=ADD,
+            )
 
         nc.vector.tensor_copy(out=bkv[:], in_=bkv_bf16[:])
         scalar_only = (nc.scalar.copy, nc.scalar.copy)
@@ -276,58 +258,50 @@ def tile_selfattention_pa_kernel(
         for first_tile in range(0, TILES, 2):
             for g in range(D_PASSES):
                 quantise_x(first_tile, 2, g, scalar_only)
-        for t in range(PACK):
-            compress(0, t)
         quantise_wv(0, shared)
         quantise_wk(0, shared)
         nc.vector.tensor_copy(out=bk[:], in_=bk_bf16[:])
-        transpose_tables()
+        for t in range(PACK):
+            compress(0, t)
         quantise_c(0)
 
         later = []
         for q in range(1, CHUNKS):
-            later.append((quantise_wk, (q, shared)))
-            later.append((quantise_wv, (q, shared)))
+            later.append((quantise_wk, (q, scalar_only)))
+            later.append((quantise_wv, (q, scalar_only)))
         for g in range(D_PASSES):
-            later.append((quantise_x, (TILES, TILES, g, shared)))
+            later.append((quantise_x, (TILES, TILES, g, scalar_only)))
         for t in range(PACK):
             later.append((compress, (1, t)))
         later.append((quantise_c, (1,)))
 
-        def finish_head(half, h, products, k_rows):
-            rope_sums(products, k_rows[:, :, h % 2, :])
-            if h % 2 == 1:
-                nc.sync.dma_start(
-                    out=out_0[half * BANK : (half + 1) * BANK, h - 1 : h + 1, :].rearrange(
-                        "(j p) h d -> p j h d", p=P
-                    ),
-                    in_=k_rows[:],
-                )
-
         steps = [(half, h) for half in range(S_HALVES) for h in range(HEADS)]
-        kT_bank_next = project_key_head(*steps[0])
-        unfinished = None
+        kT_next = project_key_head(*steps[0])
         for step, (half, h) in enumerate(steps):
             q, i = divmod(h, CHUNK_HEADS)
             j = half * TILES + i
             if h % 2 == 0:
-                k_rows = results.tile([P, TILES, 2, HEAD_DIM], F32, tag="k_rows")
+                products = results.tile([P, 2, TILES, 2, HEAD_DIM], F32, tag="products")
                 v_rows = results.tile([P, 2, BANK], F32, tag="v_rows")
-            kT_bank = kT_bank_next
+            kT = kT_next
             if step + 1 < len(steps):
-                kT_bank_next = project_key_head(*steps[step + 1])
+                kT_next = project_key_head(*steps[step + 1])
             project_values(j, q, v_rows[:, h % 2, :])
-            if unfinished is not None:
-                finish_head(*unfinished)
-            unfinished = (half, h, rope_products(half, h, kT_bank), k_rows)
+            rope_products(half, kT, products[:, :, :, h % 2, :])
             if step < len(later):
                 piece, arguments = later[step]
                 piece(*arguments)
             if h % 2 == 1:
+                rope_sums(products)
                 nc.sync.dma_start(
                     out=out_1[
                         (j - 1) * P : (j + 1) * P, q * CHUNK_HEADS : (q + 1) * CHUNK_HEADS, :
                     ].rearrange("(r p) h d -> p r (h d)", p=P),
                     in_=v_rows[:],
                 )
-        finish_head(*unfinished)
+                nc.sync.dma_start(
+                    out=out_0[half * BANK : (half + 1) * BANK, h - 1 : h + 1, :].rearrange(
+                        "(j p) h d -> p j h d", p=P
+                    ),
+                    in_=products[:, 0],
+                )

from contextlib import ExitStack

import concourse.mybir as mybir
from concourse.masks import make_identity

F32 = mybir.dt.float32
BF16 = mybir.dt.bfloat16
U32 = mybir.dt.uint32
U8 = mybir.dt.uint8
FP8X4 = mybir.dt.float8_e4m3fn_x4
ADD = mybir.AluOpType.add
SUBTRACT = mybir.AluOpType.subtract
MULT = mybir.AluOpType.mult
IDENTITY = mybir.ActivationFunctionType.Identity

P = 128
PACK = 4
K_PASS = P * PACK
WORDS = K_PASS // 2
BANK = 512

S, D, CKV, HEADS, HEAD_DIM = 1024, 2048, 512, 16, 128
E = HEADS * HEAD_DIM
HALF_DIM = HEAD_DIM // 2
S_TILES = S // P
S_HALVES = S // BANK
TILES = BANK // P
D_PASSES = D // K_PASS
CHUNKS = E // BANK
CHUNK_HEADS = BANK // HEAD_DIM

FLOPS = 2 * S * D * CKV + 2 * 2 * S * CKV * E


def quantise_rows(nc, banks, stage, identity, copies, raw_words, codes, scales):
    row_tiles = raw_words.shape[1]
    grouped = stage.tile([P, 4 * P, PACK], BF16, tag="grouped", align_bytes=64)
    grouped_words = grouped[:].bitcast(F32)
    for first in range(0, row_tiles, 2):
        bank = banks.tile([P, 2, 2, P], F32, tag="turned", bufs=4)
        for r in range(2):
            for u in range(2):
                nc.tensor.transpose(
                    bank[:, r, u, :], raw_words[:, first + r, u * P : (u + 1) * P], identity[:]
                )
        copies[first // 2](
            out=grouped_words[:, first * P : (first + 2) * P, :].rearrange(
                "p (r row) u -> p r row u", r=2
            ),
            in_=bank[:].rearrange("p r u row -> p r row u"),
        )
    nc.vector.quantize_mx(
        out=codes.bitcast(FP8X4),
        scales=scales,
        in_=grouped[:, : row_tiles * P, :].rearrange("p row t -> p (row t)"),
    )


def tile_selfattention_pa_kernel(
    tc, x, rope_cos, rope_sin, wkv_down, bkv_down, wk_up, bk_up, wv_up, bv_up, out_0, out_1
):
    nc = tc.nc
    with ExitStack() as pools:
        keep = pools.enter_context(tc.tile_pool(name="keep", bufs=1))
        stage = pools.enter_context(tc.tile_pool(name="stage", bufs=4))
        results = pools.enter_context(tc.tile_pool(name="results", bufs=4))
        banks = pools.enter_context(tc.psum_pool(name="banks", bufs=2))

        identity = keep.tile([P, P], F32)
        make_identity(nc, identity[:])

        wkv_raw = keep.tile([P, PACK, D], BF16)
        wkv_rows = wkv_down.rearrange("(u p e) d -> p u e d", u=2, e=2)
        for u in range(2):
            nc.sync.dma_start(out=wkv_raw[:, 2 * u : 2 * u + 2, :], in_=wkv_rows[:, u])
        bkv_bf16 = keep.tile([P, PACK], BF16)
        nc.sync.dma_start(
            out=bkv_bf16[:].rearrange("p (u e) -> p u e", u=2),
            in_=bkv_down.rearrange("(u p e) -> p u e", u=2, e=2),
        )

        x_raw = keep.tile([P, S_TILES, D], BF16)
        x_rows = x.rearrange("(j p) d -> p j d", p=P)
        wk_raw = keep.tile([P, HEADS, CKV], BF16)
        wk_rows = wk_up.rearrange("(h p) c -> p h c", p=P)
        wv_raw = keep.tile([P, HEADS, CKV], BF16)
        wv_rows = wv_up.rearrange("(h p) c -> p h c", p=P)

        def load_x_half(half):
            for j in range(half * TILES, (half + 1) * TILES, 2):
                nc.sync.dma_start(out=x_raw[:, j : j + 2, :], in_=x_rows[:, j : j + 2, :])

        def load_up_weights(q):
            heads = slice(q * CHUNK_HEADS, (q + 1) * CHUNK_HEADS)
            nc.sync.dma_start(out=wk_raw[:, heads, :], in_=wk_rows[:, heads, :])
            nc.sync.dma_start(out=wv_raw[:, heads, :], in_=wv_rows[:, heads, :])

        load_x_half(0)
        load_up_weights(0)
        bk_bf16 = keep.tile([P, HEADS], BF16)
        with nc.allow_non_contiguous_dma(reason="a 4 KiB bias, one element to a partition"):
            nc.sync.dma_start(out=bk_bf16[:], in_=bk_up.rearrange("(h d) -> d h", d=HEAD_DIM))
        tables = keep.tile([P, S_TILES, 2, HEAD_DIM], BF16)
        sin_raw = keep.tile([P, S_TILES, HEAD_DIM], BF16)
        nc.sync.dma_start(out=tables[:, :, 0, :], in_=rope_cos.rearrange("(j p) d -> p j d", p=P))
        nc.sync.dma_start(out=sin_raw[:], in_=rope_sin.rearrange("(j p) d -> p j d", p=P))
        nc.gpsimd.tensor_copy(out=tables[:, :, 1, :HALF_DIM], in_=sin_raw[:, :, HALF_DIM:])
        nc.gpsimd.tensor_copy(out=tables[:, :, 1, HALF_DIM:], in_=sin_raw[:, :, :HALF_DIM])
        bv_all = keep.tile([P, E], BF16)
        nc.sync.dma_start(out=bv_all[:], in_=bv_up.partition_broadcast(P))
        for q in range(1, CHUNKS):
            load_up_weights(q)
        load_x_half(1)

        wkv_codes = keep.tile([P, D_PASSES, CKV], U32, align_bytes=64)
        wkv_scales = keep.tile([P, D_PASSES, CKV], U8, align_bytes=64)
        x_codes = keep.tile([P, D_PASSES, S], U32, align_bytes=64)
        x_scales = keep.tile([P, D_PASSES, S], U8, align_bytes=64)
        c_codes = keep.tile([P, S], U32, align_bytes=64)
        c_scales = keep.tile([P, S], U8, align_bytes=64)
        wk_codes = keep.tile([P, E], U32, align_bytes=64)
        wk_scales = keep.tile([P, E], U8, align_bytes=64)
        wv_codes = keep.tile([P, E], U32, align_bytes=64)
        wv_scales = keep.tile([P, E], U8, align_bytes=64)

        wkv_words = wkv_raw[:].bitcast(F32)
        x_words = x_raw[:].bitcast(F32)
        wk_words = wk_raw[:].bitcast(F32)
        wv_words = wv_raw[:].bitcast(F32)

        def quantise_wkv(g, copies):
            quantise_rows(
                nc, banks, stage, identity, copies,
                wkv_words[:, :, g * WORDS : (g + 1) * WORDS], wkv_codes[:, g, :], wkv_scales[:, g, :],
            )

        def quantise_x(first_tile, tiles, g, copies):
            cols = slice(first_tile * P, (first_tile + tiles) * P)
            quantise_rows(
                nc, banks, stage, identity, copies,
                x_words[:, first_tile : first_tile + tiles, g * WORDS : (g + 1) * WORDS],
                x_codes[:, g, cols], x_scales[:, g, cols],
            )

        def quantise_wk(q, copies):
            cols = slice(q * BANK, (q + 1) * BANK)
            quantise_rows(
                nc, banks, stage, identity, copies,
                wk_words[:, q * CHUNK_HEADS : (q + 1) * CHUNK_HEADS, :],
                wk_codes[:, cols], wk_scales[:, cols],
            )

        def quantise_wv(q, copies):
            cols = slice(q * BANK, (q + 1) * BANK)
            quantise_rows(
                nc, banks, stage, identity, copies,
                wv_words[:, q * CHUNK_HEADS : (q + 1) * CHUNK_HEADS, :],
                wv_codes[:, cols], wv_scales[:, cols],
            )

        bkv = keep.tile([P, PACK], F32)
        bk = keep.tile([P, HEADS], F32)
        c_rows = keep.tile([P, S_HALVES, PACK, BANK], BF16)

        def compress(half, t):
            pos = slice(half * BANK, (half + 1) * BANK)
            rows = slice(t * P, (t + 1) * P)
            c_bank = banks.tile([P, BANK], F32, tag="for_scalar")
            for g in range(D_PASSES):
                nc.tensor.matmul_mx(
                    out=c_bank[:],
                    lhsT=wkv_codes[:, g, rows].bitcast(FP8X4),
                    lhsT_scale=wkv_scales[:, g, rows],
                    rhs=x_codes[:, g, pos].bitcast(FP8X4),
                    rhs_scale=x_scales[:, g, pos],
                    start=(g == 0),
                    stop=(g == D_PASSES - 1),
                )
            nc.scalar.activation(
                out=c_rows[:, half, t, :], in_=c_bank[:], func=IDENTITY, bias=bkv[:, t : t + 1],
                scale=1.0,
            )

        def quantise_c(half):
            pos = slice(half * BANK, (half + 1) * BANK)
            c_grouped = stage.tile([P, BANK, PACK], BF16, tag="grouped", align_bytes=64)
            nc.vector.tensor_copy(out=c_grouped[:], in_=c_rows[:, half].rearrange("p t s -> p s t"))
            nc.vector.quantize_mx(
                out=c_codes[:, pos].bitcast(FP8X4),
                scales=c_scales[:, pos],
                in_=c_grouped[:].rearrange("p s t -> p (s t)"),
            )

        def project_key_head(half, h):
            pos = slice(half * BANK, (half + 1) * BANK)
            cols = slice(h * HEAD_DIM, (h + 1) * HEAD_DIM)
            kT_bank = banks.tile([P, BANK], F32, tag="for_scalar")
            nc.tensor.matmul_mx(
                out=kT_bank[:],
                lhsT=wk_codes[:, cols].bitcast(FP8X4),
                lhsT_scale=wk_scales[:, cols],
                rhs=c_codes[:, pos].bitcast(FP8X4),
                rhs_scale=c_scales[:, pos],
                start=True,
                stop=True,
            )
            kT = stage.tile([P, BANK], F32, tag="kT")
            nc.scalar.activation(
                out=kT[:], in_=kT_bank[:], func=IDENTITY, bias=bk[:, h : h + 1], scale=1.0
            )
            return kT

        def project_values(j, q, v_rows):
            pos = slice(j * P, (j + 1) * P)
            cols = slice(q * BANK, (q + 1) * BANK)
            v_bank = banks.tile([P, BANK], F32, tag="for_vector")
            nc.tensor.matmul_mx(
                out=v_bank[:],
                lhsT=c_codes[:, pos].bitcast(FP8X4),
                lhsT_scale=c_scales[:, pos],
                rhs=wv_codes[:, cols].bitcast(FP8X4),
                rhs_scale=wv_scales[:, cols],
                start=True,
                stop=True,
            )
            nc.vector.tensor_tensor(out=v_rows, in0=v_bank[:], in1=bv_all[:, cols], op=ADD)

        def rope_products(half, kT, products):
            k_bank = banks.tile([P, TILES, HEAD_DIM], F32, tag="turned", bufs=4)
            for jj in range(TILES):
                nc.tensor.transpose(k_bank[:, jj, :], kT[:, jj * P : (jj + 1) * P], identity[:])
            nc.vector.tensor_tensor(
                out=products,
                in0=k_bank[:].unsqueeze(1).to_broadcast([P, 2, TILES, HEAD_DIM]),
                in1=tables[:, half * TILES : (half + 1) * TILES].rearrange("p j c d -> p c j d"),
                op=MULT,
            )

        def rope_sums(products):
            nc.gpsimd.tensor_tensor(
                out=products[:, 0, :, :, :HALF_DIM],
                in0=products[:, 0, :, :, :HALF_DIM],
                in1=products[:, 1, :, :, HALF_DIM:],
                op=SUBTRACT,
            )
            nc.gpsimd.tensor_tensor(
                out=products[:, 0, :, :, HALF_DIM:],
                in0=products[:, 0, :, :, HALF_DIM:],
                in1=products[:, 1, :, :, :HALF_DIM],
                op=ADD,
            )

        nc.vector.tensor_copy(out=bkv[:], in_=bkv_bf16[:])
        scalar_only = (nc.scalar.copy, nc.scalar.copy)
        shared = (nc.scalar.copy, nc.vector.tensor_copy)
        for g in range(D_PASSES):
            quantise_wkv(g, shared)
        for first_tile in range(0, TILES, 2):
            for g in range(D_PASSES):
                quantise_x(first_tile, 2, g, scalar_only)
        quantise_wv(0, shared)
        quantise_wk(0, shared)
        nc.vector.tensor_copy(out=bk[:], in_=bk_bf16[:])
        for t in range(PACK):
            compress(0, t)
        quantise_c(0)

        later = []
        for q in range(1, CHUNKS):
            later.append((quantise_wk, (q, scalar_only)))
            later.append((quantise_wv, (q, scalar_only)))
        for g in range(D_PASSES):
            later.append((quantise_x, (TILES, TILES, g, scalar_only)))
        for t in range(PACK):
            later.append((compress, (1, t)))
        later.append((quantise_c, (1,)))

        steps = [(half, h) for half in range(S_HALVES) for h in range(HEADS)]
        kT_next = project_key_head(*steps[0])
        for step, (half, h) in enumerate(steps):
            q, i = divmod(h, CHUNK_HEADS)
            j = half * TILES + i
            if h % 2 == 0:
                products = results.tile([P, 2, TILES, 2, HEAD_DIM], F32, tag="products")
                v_rows = results.tile([P, 2, BANK], F32, tag="v_rows")
            kT = kT_next
            if step + 1 < len(steps):
                kT_next = project_key_head(*steps[step + 1])
            project_values(j, q, v_rows[:, h % 2, :])
            rope_products(half, kT, products[:, :, :, h % 2, :])
            if step < len(later):
                piece, arguments = later[step]
                piece(*arguments)
            if h % 2 == 1:
                rope_sums(products)
                nc.sync.dma_start(
                    out=out_1[
                        (j - 1) * P : (j + 1) * P, q * CHUNK_HEADS : (q + 1) * CHUNK_HEADS, :
                    ].rearrange("(r p) h d -> p r (h d)", p=P),
                    in_=v_rows[:],
                )
                nc.sync.dma_start(
                    out=out_0[half * BANK : (half + 1) * BANK, h - 1 : h + 1, :].rearrange(
                        "(j p) h d -> p j h d", p=P
                    ),
                    in_=products[:, 0],
                )
